import numpy as np
import ml_dtypes


def mxq(x, axis, fmt="e4m3"):
    dtype, down = {"e4m3": (ml_dtypes.float8_e4m3fn, 7), "e5m2": (ml_dtypes.float8_e5m2, 14)}[fmt]
    v = np.moveaxis(np.asarray(x, np.float32).astype(ml_dtypes.bfloat16).astype(np.float64), axis, -1)
    blocks = v.reshape(v.shape[:-1] + (-1, 32))
    amax = np.abs(blocks).max(-1, keepdims=True)
    byte = np.maximum(np.where(amax > 0, np.frexp(amax)[1] - 1 + 127, 0) - down, 1)
    scale = np.exp2(byte - 127.0)
    codes = (blocks / scale).astype(np.float32).astype(dtype).astype(np.float64)
    return np.moveaxis((codes * scale).reshape(v.shape), -1, axis)


WIDE = False


def mx_kscale(k):
    if not WIDE:
        return np.ones(k)
    levels = np.array([10, -10, 5, -5, 0])
    a = np.random.permutation(np.resize(levels, k // 512 * 4)).reshape(k // 512, 4)
    idx = np.arange(k)
    return np.exp2(a[idx // 512, idx % 128 // 32])


BF16 = ml_dtypes.bfloat16


def bf(x):
    return np.asarray(x, np.float32).astype(BF16)


def f64(x):
    return np.asarray(x).astype(np.float64)


B, IN, H, OUT, L, STEPS = 4096, 512, 512, 128, 3, 3
LN_EPS = 1e-5


def layer_norm(v, g, b):
    m = v.mean(-1, keepdims=True)
    var = ((v - m) ** 2).mean(-1, keepdims=True)
    return (v - m) / np.sqrt(var + LN_EPS) * g + b


def setup_inputs():
    s = mx_kscale(H)
    s = s / s.max()
    return {"h": bf(np.random.standard_normal((B, H)) * s),
            "W_liq": bf(np.random.standard_normal((L, H, H)) / np.sqrt(H) / s),
            "b_liq": bf(np.random.standard_normal((L, H)) * 0.3),
            "g_liq": bf(1.0 + 0.1 * np.random.standard_normal((L, H))),
            "beta_liq": bf(np.random.standard_normal((L, H)) * 0.3)}


def reference(h, W_liq, b_liq, g_liq, beta_liq):
    h = f64(h)
    lin = mxq(h, 1, "e4m3") @ mxq(f64(W_liq), 2, "e4m3").transpose(0, 2, 1)
    pre = h[None] + lin + f64(b_liq)[:, None, :]
    return layer_norm(pre, f64(g_liq)[:, None, :], f64(beta_liq)[:, None, :]).sum(0)

@@ -1,0 +1,202 @@
+import concourse.mybir as mybir
+from concourse.masks import make_identity
+
+F32 = mybir.dt.float32
+BF16 = mybir.dt.bfloat16
+U32 = mybir.dt.uint32
+U8 = mybir.dt.uint8
+FP8X4 = mybir.dt.float8_e4m3fn_x4
+ALU = mybir.AluOpType
+ACT = mybir.ActivationFunctionType
+
+P = 128
+ROWS = 4096
+H = 512
+BRANCHES = 3
+TILES = ROWS // P
+O_CHUNKS = H // P
+WORDS = H // 2
+LOAD_TILES = 8
+STORE_TILES = 4
+LN_EPS = 1e-5
+
+FLOPS = 2 * ROWS * H * H * BRANCHES
+
+
+def transpose_words(nc, bank, column, words, ident):
+    for u in range(2):
+        nc.tensor.transpose(
+            bank[:, u, column : column + P], words[:, u * P : (u + 1) * P], ident[:]
+        )
+
+
+def tile_advancedliquidneuralnetwork_pa_t_kernel(
+    tc, h, W_liq, b_liq, g_liq, beta_liq, out
+):
+    nc = tc.nc
+    h_view = h.rearrange("(p j) k -> p j k", j=TILES)
+    out_view = out.rearrange("(p j) o -> p j o", j=TILES)
+
+    with tc.tile_pool(name="keep", bufs=1) as keep, tc.tile_pool(
+        name="stage", bufs=2
+    ) as stage, tc.tile_pool(name="work", bufs=3) as work, tc.tile_pool(
+        name="small", bufs=4
+    ) as small, tc.psum_pool(name="flip", bufs=2) as flip, tc.psum_pool(
+        name="prod", bufs=4
+    ) as prod:
+        w_rows = keep.tile([P, BRANCHES * O_CHUNKS, H], BF16)
+        h_rows = keep.tile([P, TILES, H], BF16)
+        w_view = W_liq.rearrange("l (c p) k -> p (l c) k", p=P)
+        nc.sync.dma_start(out=w_rows[:, 0:O_CHUNKS, :], in_=w_view[:, 0:O_CHUNKS, :])
+        nc.sync.dma_start(out=h_rows[:, 0:LOAD_TILES, :], in_=h_view[:, 0:LOAD_TILES, :])
+        nc.sync.dma_start(
+            out=w_rows[:, O_CHUNKS:, :], in_=w_view[:, O_CHUNKS:, :]
+        )
+        for j0 in range(LOAD_TILES, TILES, LOAD_TILES):
+            nc.sync.dma_start(
+                out=h_rows[:, j0 : j0 + LOAD_TILES, :], in_=h_view[:, j0 : j0 + LOAD_TILES, :]
+            )
+        bias_all = keep.tile([P, BRANCHES, H], BF16)
+        gain_all = keep.tile([P, BRANCHES, H], BF16)
+        shift_all = keep.tile([P, BRANCHES, H], BF16)
+        for vec_tile, vec in ((bias_all, b_liq), (gain_all, g_liq), (shift_all, beta_liq)):
+            nc.scalar.dma_start(
+                out=vec_tile[:].rearrange("p l o -> p (l o)"),
+                in_=vec.rearrange("l o -> (l o)").partition_broadcast(P),
+            )
+
+        ident = keep.tile([P, P], F32)
+        make_identity(nc, ident[:])
+        eps = keep.tile([P, 1], F32)
+        nc.vector.memset(eps[:], LN_EPS)
+
+        shift_sum = keep.tile([P, H], F32)
+        nc.vector.tensor_tensor(
+            out=shift_sum[:], in0=shift_all[:, 0, :], in1=shift_all[:, 1, :], op=ALU.add
+        )
+        nc.vector.tensor_tensor(
+            out=shift_sum[:], in0=shift_sum[:], in1=shift_all[:, 2, :], op=ALU.add
+        )
+
+        w_words = w_rows[:].bitcast(F32)
+        w_codes = keep.tile([P, BRANCHES, H], U32, align_bytes=64)
+        w_scales = keep.tile([P, BRANCHES, H], U8, align_bytes=64)
+        for l in range(BRANCHES):
+            w_grouped = stage.tile([P, H, 4], BF16, align_bytes=64)
+            w_grouped_words = w_grouped[:].bitcast(F32)
+            for half in range(2):
+                w_bank = flip.tile([P, 2, 2 * P], F32, tag="bank")
+                for c in range(2):
+                    transpose_words(
+                        nc, w_bank, c * P, w_words[:, l * O_CHUNKS + 2 * half + c, :], ident
+                    )
+                nc.scalar.copy(
+                    out=w_grouped_words[:, half * 2 * P : (half + 1) * 2 * P, :],
+                    in_=w_bank[:].rearrange("p u o -> p o u"),
+                )
+            nc.vector.quantize_mx(
+                out=w_codes[:, l, :].bitcast(FP8X4),
+                scales=w_scales[:, l, :],
+                in_=w_grouped[:].rearrange("p o t -> p (o t)"),
+            )
+
+        h_words = h_rows[:].bitcast(F32)
+        h_codes = keep.tile([P, TILES * P], U32, align_bytes=64)
+        h_scales = keep.tile([P, TILES * P], U8, align_bytes=64)
+
+        def quantise_two_tiles(j0):
+            h_bank = flip.tile([P, 2, 2 * P], F32, tag="bank")
+            for c in range(2):
+                transpose_words(nc, h_bank, c * P, h_words[:, j0 + c, :], ident)
+            h_grouped = stage.tile([P, 2 * P, 4], BF16, align_bytes=64)
+            nc.scalar.copy(
+                out=h_grouped[:].bitcast(F32), in_=h_bank[:].rearrange("p u r -> p r u")
+            )
+            nc.vector.quantize_mx(
+                out=h_codes[:, j0 * P : (j0 + 2) * P].bitcast(FP8X4),
+                scales=h_scales[:, j0 * P : (j0 + 2) * P],
+                in_=h_grouped[:].rearrange("p r t -> p (r t)"),
+            )
+
+        for j in range(TILES):
+            if j % 2 == 0:
+                quantise_two_tiles(j)
+            if j % STORE_TILES == 0:
+                result = work.tile([P, STORE_TILES, H], F32)
+
+            resid = work.tile([P, BRANCHES, H], F32)
+            nc.gpsimd.tensor_tensor(
+                out=resid[:],
+                in0=h_rows[:, j, :].unsqueeze(1).to_broadcast([P, BRANCHES, H]),
+                in1=bias_all[:],
+                op=ALU.add,
+            )
+
+            pre = work.tile([P, BRANCHES, H], F32)
+            row_sum = small.tile([P, BRANCHES], F32)
+            for l in range(BRANCHES):
+                lin = prod.tile([P, H], F32)
+                nc.tensor.matmul_mx(
+                    out=lin[:],
+                    lhsT=h_codes[:, j * P : (j + 1) * P].bitcast(FP8X4),
+                    lhsT_scale=h_scales[:, j * P : (j + 1) * P],
+                    rhs=w_codes[:, l, :].bitcast(FP8X4),
+                    rhs_scale=w_scales[:, l, :],
+                    start=True,
+                    stop=True,
+                )
+                nc.vector.scalar_tensor_tensor(
+                    out=pre[:, l, :],
+                    in0=lin[:],
+                    scalar=0.0,
+                    in1=resid[:, l, :],
+                    op0=ALU.add,
+                    op1=ALU.add,
+                    accum_out=row_sum[:, l : l + 1],
+                )
+
+            neg_mean = small.tile([P, BRANCHES], F32)
+            nc.vector.tensor_scalar_mul(out=neg_mean[:], in0=row_sum[:], scalar1=-1.0 / H)
+
+            sq_sum = small.tile([P, BRANCHES], F32)
+            for l in range(BRANCHES):
+                squares = work.tile([P, H], F32)
+                nc.scalar.activation(
+                    out=squares[:],
+                    in_=pre[:, l, :],
+                    func=ACT.Square,
+                    bias=neg_mean[:, l : l + 1],
+                    scale=1.0,
+                    accum_out=sq_sum[:, l : l + 1],
+                )
+            std = small.tile([P, BRANCHES], F32)
+            nc.scalar.activation(
+                out=std[:], in_=sq_sum[:], func=ACT.Sqrt, bias=eps[:], scale=1.0 / H
+            )
+            inv_std = small.tile([P, BRANCHES], F32)
+            nc.vector.reciprocal(out=inv_std[:], in_=std[:])
+
+            total = shift_sum[:]
+            for l in range(BRANCHES):
+                gained = work.tile([P, H], F32)
+                nc.vector.scalar_tensor_tensor(
+                    out=gained[:],
+                    in0=pre[:, l, :],
+                    scalar=neg_mean[:, l : l + 1],
+                    in1=gain_all[:, l, :],
+                    op0=ALU.add,
+                    op1=ALU.mult,
+                )
+                nc.vector.scalar_tensor_tensor(
+                    out=result[:, j % STORE_TILES, :],
+                    in0=gained[:],
+                    scalar=inv_std[:, l : l + 1],
+                    in1=total,
+                    op0=ALU.mult,
+                    op1=ALU.add,
+                )
+                total = result[:, j % STORE_TILES, :]
+
+            if j % STORE_TILES == STORE_TILES - 1:
+                j0 = j - (STORE_TILES - 1)
+                nc.sync.dma_start(out=out_view[:, j0 : j + 1, :], in_=result[:])

@@ -14,10 +14,9 @@ ROWS = 4096
 H = 512
 BRANCHES = 3
 TILES = ROWS // P
-O_CHUNKS = H // P
-WORDS = H // 2
+CHUNKS = H // P
+QUAD = 4
 LOAD_TILES = 8
-STORE_TILES = 4
 LN_EPS = 1e-5
 
 FLOPS = 2 * ROWS * H * H * BRANCHES
@@ -40,42 +39,60 @@ def tile_advancedliquidneuralnetwork_pa_t_kernel(
     with tc.tile_pool(name="keep", bufs=1) as keep, tc.tile_pool(
         name="stage", bufs=2
     ) as stage, tc.tile_pool(name="work", bufs=3) as work, tc.tile_pool(
-        name="small", bufs=4
-    ) as small, tc.psum_pool(name="flip", bufs=2) as flip, tc.psum_pool(
-        name="prod", bufs=4
-    ) as prod:
-        w_rows = keep.tile([P, BRANCHES * O_CHUNKS, H], BF16)
+        name="quads", bufs=2
+    ) as quads, tc.tile_pool(name="small", bufs=6) as small, tc.psum_pool(
+        name="flip", bufs=2
+    ) as flip, tc.psum_pool(name="prod", bufs=2) as prod, tc.psum_pool(
+        name="cols", bufs=4
+    ) as cols:
+        w_rows = keep.tile([P, BRANCHES * CHUNKS, H], BF16)
         h_rows = keep.tile([P, TILES, H], BF16)
         w_view = W_liq.rearrange("l (c p) k -> p (l c) k", p=P)
-        nc.sync.dma_start(out=w_rows[:, 0:O_CHUNKS, :], in_=w_view[:, 0:O_CHUNKS, :])
+        nc.sync.dma_start(out=w_rows[:, 0:CHUNKS, :], in_=w_view[:, 0:CHUNKS, :])
         nc.sync.dma_start(out=h_rows[:, 0:LOAD_TILES, :], in_=h_view[:, 0:LOAD_TILES, :])
-        nc.sync.dma_start(
-            out=w_rows[:, O_CHUNKS:, :], in_=w_view[:, O_CHUNKS:, :]
-        )
+        nc.sync.dma_start(out=w_rows[:, CHUNKS:, :], in_=w_view[:, CHUNKS:, :])
         for j0 in range(LOAD_TILES, TILES, LOAD_TILES):
             nc.sync.dma_start(
                 out=h_rows[:, j0 : j0 + LOAD_TILES, :], in_=h_view[:, j0 : j0 + LOAD_TILES, :]
             )
         bias_all = keep.tile([P, BRANCHES, H], BF16)
-        gain_all = keep.tile([P, BRANCHES, H], BF16)
-        shift_all = keep.tile([P, BRANCHES, H], BF16)
-        for vec_tile, vec in ((bias_all, b_liq), (gain_all, g_liq), (shift_all, beta_liq)):
-            nc.scalar.dma_start(
-                out=vec_tile[:].rearrange("p l o -> p (l o)"),
-                in_=vec.rearrange("l o -> (l o)").partition_broadcast(P),
-            )
+        nc.scalar.dma_start(
+            out=bias_all[:].rearrange("p l o -> p (l o)"),
+            in_=b_liq.rearrange("l o -> (l o)").partition_broadcast(P),
+        )
+        VECS = BRANCHES * CHUNKS
+        vec_rows = keep.tile([P, P], BF16)
+        nc.vector.memset(vec_rows[:], 0.0)
+        nc.scalar.dma_start(
+            out=vec_rows[0:VECS, :], in_=g_liq.rearrange("l (c p) -> (l c) p", p=P)
+        )
+        nc.scalar.dma_start(
+            out=vec_rows[VECS : 2 * VECS, :], in_=beta_liq.rearrange("l (c p) -> (l c) p", p=P)
+        )
 
         ident = keep.tile([P, P], F32)
         make_identity(nc, ident[:])
         eps = keep.tile([P, 1], F32)
         nc.vector.memset(eps[:], LN_EPS)
 
-        shift_sum = keep.tile([P, H], F32)
+        vec_rows_f32 = keep.tile([P, P], F32)
+        nc.vector.tensor_copy(out=vec_rows_f32[:], in_=vec_rows[:])
+        vec_bank = flip.tile([P, P], F32, tag="bank")
+        nc.tensor.transpose(vec_bank[:], vec_rows_f32[:], ident[:])
+        vec_cols = keep.tile([P, P], F32)
+        nc.vector.tensor_copy(out=vec_cols[:], in_=vec_bank[:])
+        shift_cols = keep.tile([P, CHUNKS], F32)
         nc.vector.tensor_tensor(
-            out=shift_sum[:], in0=shift_all[:, 0, :], in1=shift_all[:, 1, :], op=ALU.add
+            out=shift_cols[:],
+            in0=vec_cols[:, VECS : VECS + CHUNKS],
+            in1=vec_cols[:, VECS + CHUNKS : VECS + 2 * CHUNKS],
+            op=ALU.add,
         )
         nc.vector.tensor_tensor(
-            out=shift_sum[:], in0=shift_sum[:], in1=shift_all[:, 2, :], op=ALU.add
+            out=shift_cols[:],
+            in0=shift_cols[:],
+            in1=vec_cols[:, VECS + 2 * CHUNKS : VECS + 3 * CHUNKS],
+            op=ALU.add,
         )
 
         w_words = w_rows[:].bitcast(F32)
@@ -88,7 +105,7 @@ def tile_advancedliquidneuralnetwork_pa_t_kernel(
                 w_bank = flip.tile([P, 2, 2 * P], F32, tag="bank")
                 for c in range(2):
                     transpose_words(
-                        nc, w_bank, c * P, w_words[:, l * O_CHUNKS + 2 * half + c, :], ident
+                        nc, w_bank, c * P, w_words[:, l * CHUNKS + 2 * half + c, :], ident
                     )
                 nc.scalar.copy(
                     out=w_grouped_words[:, half * 2 * P : (half + 1) * 2 * P, :],
@@ -118,12 +135,7 @@ def tile_advancedliquidneuralnetwork_pa_t_kernel(
                 in_=h_grouped[:].rearrange("p r t -> p (r t)"),
             )
 
-        for j in range(TILES):
-            if j % 2 == 0:
-                quantise_two_tiles(j)
-            if j % STORE_TILES == 0:
-                result = work.tile([P, STORE_TILES, H], F32)
-
+        def normalised_branches(j, normed):
             resid = work.tile([P, BRANCHES, H], F32)
             nc.gpsimd.tensor_tensor(
                 out=resid[:],
@@ -131,8 +143,6 @@ def tile_advancedliquidneuralnetwork_pa_t_kernel(
                 in1=bias_all[:],
                 op=ALU.add,
             )
-
-            pre = work.tile([P, BRANCHES, H], F32)
             row_sum = small.tile([P, BRANCHES], F32)
             for l in range(BRANCHES):
                 lin = prod.tile([P, H], F32)
@@ -146,7 +156,7 @@ def tile_advancedliquidneuralnetwork_pa_t_kernel(
                     stop=True,
                 )
                 nc.vector.scalar_tensor_tensor(
-                    out=pre[:, l, :],
+                    out=normed[:, l, :],
                     in0=lin[:],
                     scalar=0.0,
                     in1=resid[:, l, :],
@@ -154,16 +164,14 @@ def tile_advancedliquidneuralnetwork_pa_t_kernel(
                     op1=ALU.add,
                     accum_out=row_sum[:, l : l + 1],
                 )
-
             neg_mean = small.tile([P, BRANCHES], F32)
             nc.vector.tensor_scalar_mul(out=neg_mean[:], in0=row_sum[:], scalar1=-1.0 / H)
-
             sq_sum = small.tile([P, BRANCHES], F32)
             for l in range(BRANCHES):
                 squares = work.tile([P, H], F32)
                 nc.scalar.activation(
                     out=squares[:],
-                    in_=pre[:, l, :],
+                    in_=normed[:, l, :],
                     func=ACT.Square,
                     bias=neg_mean[:, l : l + 1],
                     scale=1.0,
@@ -175,28 +183,60 @@ def tile_advancedliquidneuralnetwork_pa_t_kernel(
             )
             inv_std = small.tile([P, BRANCHES], F32)
             nc.vector.reciprocal(out=inv_std[:], in_=std[:])
-
-            total = shift_sum[:]
+            offset = small.tile([P, BRANCHES], F32)
+            nc.vector.tensor_tensor(out=offset[:], in0=neg_mean[:], in1=inv_std[:], op=ALU.mult)
             for l in range(BRANCHES):
-                gained = work.tile([P, H], F32)
-                nc.vector.scalar_tensor_tensor(
-                    out=gained[:],
-                    in0=pre[:, l, :],
-                    scalar=neg_mean[:, l : l + 1],
-                    in1=gain_all[:, l, :],
-                    op0=ALU.add,
-                    op1=ALU.mult,
+                nc.scalar.activation(
+                    out=normed[:, l, :],
+                    in_=normed[:, l, :],
+                    func=ACT.Identity,
+                    bias=offset[:, l : l + 1],
+                    scale=inv_std[:, l : l + 1],
                 )
-                nc.vector.scalar_tensor_tensor(
-                    out=result[:, j % STORE_TILES, :],
-                    in0=gained[:],
-                    scalar=inv_std[:, l : l + 1],
-                    in1=total,
-                    op0=ALU.mult,
-                    op1=ALU.add,
-                )
-                total = result[:, j % STORE_TILES, :]
 
-            if j % STORE_TILES == STORE_TILES - 1:
-                j0 = j - (STORE_TILES - 1)
-                nc.sync.dma_start(out=out_view[:, j0 : j + 1, :], in_=result[:])
+        for j0 in range(0, TILES, QUAD):
+            normed = quads.tile([P, QUAD, BRANCHES, H], F32)
+            for q in range(QUAD):
+                if q % 2 == 0:
+                    quantise_two_tiles(j0 + q)
+                normalised_branches(j0 + q, normed[:, q, :, :])
+
+            summed = quads.tile([P, CHUNKS, QUAD * P], F32)
+            for l in range(BRANCHES):
+                for c in range(CHUNKS):
+                    flipped = cols.tile([P, QUAD * P], F32)
+                    for q in range(QUAD):
+                        nc.tensor.transpose(
+                            flipped[:, q * P : (q + 1) * P],
+                            normed[:, q, l, c * P : (c + 1) * P],
+                            ident[:],
+                        )
+                    gain = vec_cols[:, l * CHUNKS + c : l * CHUNKS + c + 1]
+                    if l == 0:
+                        nc.vector.tensor_scalar(
+                            out=summed[:, c, :],
+                            in0=flipped[:],
+                            scalar1=gain,
+                            scalar2=shift_cols[:, c : c + 1],
+                            op0=ALU.mult,
+                            op1=ALU.add,
+                        )
+                    else:
+                        nc.vector.scalar_tensor_tensor(
+                            out=summed[:, c, :],
+                            in0=flipped[:],
+                            scalar=gain,
+                            in1=summed[:, c, :],
+                            op0=ALU.mult,
+                            op1=ALU.add,
+                        )
+
+            result = quads.tile([P, QUAD, H], F32)
+            for q in range(QUAD):
+                back = flip.tile([P, H], F32, tag="bank")
+                for c in range(CHUNKS):
+                    nc.tensor.transpose(
+                        back[:, c * P : (c + 1) * P], summed[:, c, q * P : (q + 1) * P], ident[:]
+                    )
+                nc.vector.tensor_copy(out=result[:, q, :], in_=back[:])
+            nc.sync.dma_start(out=out_view[:, j0 : j0 + QUAD, :], in_=result[:])

@@ -14,9 +14,10 @@ ROWS = 4096
 H = 512
 BRANCHES = 3
 TILES = ROWS // P
-CHUNKS = H // P
-QUAD = 4
+O_CHUNKS = H // P
+WORDS = H // 2
 LOAD_TILES = 8
+STORE_TILES = 4
 LN_EPS = 1e-5
 
 FLOPS = 2 * ROWS * H * H * BRANCHES
@@ -39,60 +40,42 @@ def tile_advancedliquidneuralnetwork_pa_t_kernel(
     with tc.tile_pool(name="keep", bufs=1) as keep, tc.tile_pool(
         name="stage", bufs=2
     ) as stage, tc.tile_pool(name="work", bufs=3) as work, tc.tile_pool(
-        name="quads", bufs=2
-    ) as quads, tc.tile_pool(name="small", bufs=6) as small, tc.psum_pool(
-        name="flip", bufs=2
-    ) as flip, tc.psum_pool(name="prod", bufs=2) as prod, tc.psum_pool(
-        name="cols", bufs=4
-    ) as cols:
-        w_rows = keep.tile([P, BRANCHES * CHUNKS, H], BF16)
+        name="small", bufs=4
+    ) as small, tc.psum_pool(name="flip", bufs=2) as flip, tc.psum_pool(
+        name="prod", bufs=4
+    ) as prod:
+        w_rows = keep.tile([P, BRANCHES * O_CHUNKS, H], BF16)
         h_rows = keep.tile([P, TILES, H], BF16)
         w_view = W_liq.rearrange("l (c p) k -> p (l c) k", p=P)
-        nc.sync.dma_start(out=w_rows[:, 0:CHUNKS, :], in_=w_view[:, 0:CHUNKS, :])
+        nc.sync.dma_start(out=w_rows[:, 0:O_CHUNKS, :], in_=w_view[:, 0:O_CHUNKS, :])
         nc.sync.dma_start(out=h_rows[:, 0:LOAD_TILES, :], in_=h_view[:, 0:LOAD_TILES, :])
-        nc.sync.dma_start(out=w_rows[:, CHUNKS:, :], in_=w_view[:, CHUNKS:, :])
+        nc.sync.dma_start(
+            out=w_rows[:, O_CHUNKS:, :], in_=w_view[:, O_CHUNKS:, :]
+        )
         for j0 in range(LOAD_TILES, TILES, LOAD_TILES):
             nc.sync.dma_start(
                 out=h_rows[:, j0 : j0 + LOAD_TILES, :], in_=h_view[:, j0 : j0 + LOAD_TILES, :]
             )
         bias_all = keep.tile([P, BRANCHES, H], BF16)
-        nc.scalar.dma_start(
-            out=bias_all[:].rearrange("p l o -> p (l o)"),
-            in_=b_liq.rearrange("l o -> (l o)").partition_broadcast(P),
-        )
-        VECS = BRANCHES * CHUNKS
-        vec_rows = keep.tile([P, P], BF16)
-        nc.vector.memset(vec_rows[:], 0.0)
-        nc.scalar.dma_start(
-            out=vec_rows[0:VECS, :], in_=g_liq.rearrange("l (c p) -> (l c) p", p=P)
-        )
-        nc.scalar.dma_start(
-            out=vec_rows[VECS : 2 * VECS, :], in_=beta_liq.rearrange("l (c p) -> (l c) p", p=P)
-        )
+        gain_all = keep.tile([P, BRANCHES, H], BF16)
+        shift_all = keep.tile([P, BRANCHES, H], BF16)
+        for vec_tile, vec in ((bias_all, b_liq), (gain_all, g_liq), (shift_all, beta_liq)):
+            nc.scalar.dma_start(
+                out=vec_tile[:].rearrange("p l o -> p (l o)"),
+                in_=vec.rearrange("l o -> (l o)").partition_broadcast(P),
+            )
 
         ident = keep.tile([P, P], F32)
         make_identity(nc, ident[:])
         eps = keep.tile([P, 1], F32)
         nc.vector.memset(eps[:], LN_EPS)
 
-        vec_rows_f32 = keep.tile([P, P], F32)
-        nc.vector.tensor_copy(out=vec_rows_f32[:], in_=vec_rows[:])
-        vec_bank = flip.tile([P, P], F32, tag="bank")
-        nc.tensor.transpose(vec_bank[:], vec_rows_f32[:], ident[:])
-        vec_cols = keep.tile([P, P], F32)
-        nc.vector.tensor_copy(out=vec_cols[:], in_=vec_bank[:])
-        shift_cols = keep.tile([P, CHUNKS], F32)
+        shift_sum = keep.tile([P, H], F32)
         nc.vector.tensor_tensor(
-            out=shift_cols[:],
-            in0=vec_cols[:, VECS : VECS + CHUNKS],
-            in1=vec_cols[:, VECS + CHUNKS : VECS + 2 * CHUNKS],
-            op=ALU.add,
+            out=shift_sum[:], in0=shift_all[:, 0, :], in1=shift_all[:, 1, :], op=ALU.add
         )
         nc.vector.tensor_tensor(
-            out=shift_cols[:],
-            in0=shift_cols[:],
-            in1=vec_cols[:, VECS + 2 * CHUNKS : VECS + 3 * CHUNKS],
-            op=ALU.add,
+            out=shift_sum[:], in0=shift_sum[:], in1=shift_all[:, 2, :], op=ALU.add
         )
 
         w_words = w_rows[:].bitcast(F32)
@@ -105,7 +88,7 @@ def tile_advancedliquidneuralnetwork_pa_t_kernel(
                 w_bank = flip.tile([P, 2, 2 * P], F32, tag="bank")
                 for c in range(2):
                     transpose_words(
-                        nc, w_bank, c * P, w_words[:, l * CHUNKS + 2 * half + c, :], ident
+                        nc, w_bank, c * P, w_words[:, l * O_CHUNKS + 2 * half + c, :], ident
                     )
                 nc.scalar.copy(
                     out=w_grouped_words[:, half * 2 * P : (half + 1) * 2 * P, :],
@@ -135,14 +118,21 @@ def tile_advancedliquidneuralnetwork_pa_t_kernel(
                 in_=h_grouped[:].rearrange("p r t -> p (r t)"),
             )
 
-        def normalised_branches(j, normed):
+        for j in range(TILES):
+            if j % 2 == 0:
+                quantise_two_tiles(j)
+            if j % STORE_TILES == 0:
+                result = work.tile([P, STORE_TILES, H], F32)
+
             resid = work.tile([P, BRANCHES, H], F32)
-            nc.gpsimd.tensor_tensor(
+            nc.vector.tensor_tensor(
                 out=resid[:],
                 in0=h_rows[:, j, :].unsqueeze(1).to_broadcast([P, BRANCHES, H]),
                 in1=bias_all[:],
                 op=ALU.add,
             )
+
+            pre = work.tile([P, BRANCHES, H], F32)
             row_sum = small.tile([P, BRANCHES], F32)
             for l in range(BRANCHES):
                 lin = prod.tile([P, H], F32)
@@ -156,7 +146,7 @@ def tile_advancedliquidneuralnetwork_pa_t_kernel(
                     stop=True,
                 )
                 nc.vector.scalar_tensor_tensor(
-                    out=normed[:, l, :],
+                    out=pre[:, l, :],
                     in0=lin[:],
                     scalar=0.0,
                     in1=resid[:, l, :],
@@ -164,14 +154,16 @@ def tile_advancedliquidneuralnetwork_pa_t_kernel(
                     op1=ALU.add,
                     accum_out=row_sum[:, l : l + 1],
                 )
+
             neg_mean = small.tile([P, BRANCHES], F32)
             nc.vector.tensor_scalar_mul(out=neg_mean[:], in0=row_sum[:], scalar1=-1.0 / H)
+
             sq_sum = small.tile([P, BRANCHES], F32)
             for l in range(BRANCHES):
                 squares = work.tile([P, H], F32)
                 nc.scalar.activation(
                     out=squares[:],
-                    in_=normed[:, l, :],
+                    in_=pre[:, l, :],
                     func=ACT.Square,
                     bias=neg_mean[:, l : l + 1],
                     scale=1.0,
@@ -183,60 +175,28 @@ def tile_advancedliquidneuralnetwork_pa_t_kernel(
             )
             inv_std = small.tile([P, BRANCHES], F32)
             nc.vector.reciprocal(out=inv_std[:], in_=std[:])
-            offset = small.tile([P, BRANCHES], F32)
-            nc.vector.tensor_tensor(out=offset[:], in0=neg_mean[:], in1=inv_std[:], op=ALU.mult)
+
+            total = shift_sum[:]
             for l in range(BRANCHES):
-                nc.scalar.activation(
-                    out=normed[:, l, :],
-                    in_=normed[:, l, :],
-                    func=ACT.Identity,
-                    bias=offset[:, l : l + 1],
-                    scale=inv_std[:, l : l + 1],
+                gained = work.tile([P, H], F32)
+                nc.vector.scalar_tensor_tensor(
+                    out=gained[:],
+                    in0=pre[:, l, :],
+                    scalar=neg_mean[:, l : l + 1],
+                    in1=gain_all[:, l, :],
+                    op0=ALU.add,
+                    op1=ALU.mult,
                 )
+                nc.vector.scalar_tensor_tensor(
+                    out=result[:, j % STORE_TILES, :],
+                    in0=gained[:],
+                    scalar=inv_std[:, l : l + 1],
+                    in1=total,
+                    op0=ALU.mult,
+                    op1=ALU.add,
+                )
+                total = result[:, j % STORE_TILES, :]
 
-        for j0 in range(0, TILES, QUAD):
-            normed = quads.tile([P, QUAD, BRANCHES, H], F32)
-            for q in range(QUAD):
-                if q % 2 == 0:
-                    quantise_two_tiles(j0 + q)
-                normalised_branches(j0 + q, normed[:, q, :, :])
-
-            summed = quads.tile([P, CHUNKS, QUAD * P], F32)
-            for l in range(BRANCHES):
-                for c in range(CHUNKS):
-                    flipped = cols.tile([P, QUAD * P], F32)
-                    for q in range(QUAD):
-                        nc.tensor.transpose(
-                            flipped[:, q * P : (q + 1) * P],
-                            normed[:, q, l, c * P : (c + 1) * P],
-                            ident[:],
-                        )
-                    gain = vec_cols[:, l * CHUNKS + c : l * CHUNKS + c + 1]
-                    if l == 0:
-                        nc.vector.tensor_scalar(
-                            out=summed[:, c, :],
-                            in0=flipped[:],
-                            scalar1=gain,
-                            scalar2=shift_cols[:, c : c + 1],
-                            op0=ALU.mult,
-                            op1=ALU.add,
-                        )
-                    else:
-                        nc.vector.scalar_tensor_tensor(
-                            out=summed[:, c, :],
-                            in0=flipped[:],
-                            scalar=gain,
-                            in1=summed[:, c, :],
-                            op0=ALU.mult,
-                            op1=ALU.add,
-                        )
-
-            result = quads.tile([P, QUAD, H], F32)
-            for q in range(QUAD):
-                back = flip.tile([P, H], F32, tag="bank")
-                for c in range(CHUNKS):
-                    nc.tensor.transpose(
-                        back[:, c * P : (c + 1) * P], summed[:, c, q * P : (q + 1) * P], ident[:]
-                    )
-                nc.vector.tensor_copy(out=result[:, q, :], in_=back[:])
-            nc.sync.dma_start(out=out_view[:, j0 : j0 + QUAD, :], in_=result[:])
+            if j % STORE_TILES == STORE_TILES - 1:
+                j0 = j - (STORE_TILES - 1)
+                nc.sync.dma_start(out=out_view[:, j0 : j + 1, :], in_=result[:])

@@ -14,10 +14,15 @@ ROWS = 4096
 H = 512
 BRANCHES = 3
 TILES = ROWS // P
-O_CHUNKS = H // P
-WORDS = H // 2
+CHUNKS = H // P
+QUAD = 4
 LOAD_TILES = 8
-STORE_TILES = 4
+UNITS = BRANCHES * CHUNKS
+UNITS_PER_STEP = UNITS // QUAD
+NORM_LAG = 2
+FLIP_LAG = QUAD - 1 + NORM_LAG + 1
+BACK_LAG = FLIP_LAG + QUAD
+STEPS = TILES + BACK_LAG
 LN_EPS = 1e-5
 
 FLOPS = 2 * ROWS * H * H * BRANCHES
@@ -38,57 +43,53 @@ def tile_advancedliquidneuralnetwork_pa_t_kernel(
     out_view = out.rearrange("(p j) o -> p j o", j=TILES)
 
     with tc.tile_pool(name="keep", bufs=1) as keep, tc.tile_pool(
-        name="stage", bufs=2
-    ) as stage, tc.tile_pool(name="work", bufs=3) as work, tc.tile_pool(
-        name="small", bufs=4
+        name="pairs", bufs=2
+    ) as pairs, tc.tile_pool(name="triples", bufs=3) as triples, tc.tile_pool(
+        name="small", bufs=6
     ) as small, tc.psum_pool(name="flip", bufs=2) as flip, tc.psum_pool(
-        name="prod", bufs=4
-    ) as prod:
-        w_rows = keep.tile([P, BRANCHES * O_CHUNKS, H], BF16)
+        name="prod", bufs=BRANCHES
+    ) as prod, tc.psum_pool(name="cols", bufs=UNITS_PER_STEP) as cols, tc.manual_schedule():
+        w_rows = keep.tile([P, UNITS, H], BF16)
         h_rows = keep.tile([P, TILES, H], BF16)
         w_view = W_liq.rearrange("l (c p) k -> p (l c) k", p=P)
-        nc.sync.dma_start(out=w_rows[:, 0:O_CHUNKS, :], in_=w_view[:, 0:O_CHUNKS, :])
+        nc.sync.dma_start(out=w_rows[:, 0:CHUNKS, :], in_=w_view[:, 0:CHUNKS, :])
         nc.sync.dma_start(out=h_rows[:, 0:LOAD_TILES, :], in_=h_view[:, 0:LOAD_TILES, :])
-        nc.sync.dma_start(
-            out=w_rows[:, O_CHUNKS:, :], in_=w_view[:, O_CHUNKS:, :]
-        )
+        nc.sync.dma_start(out=w_rows[:, CHUNKS:, :], in_=w_view[:, CHUNKS:, :])
         for j0 in range(LOAD_TILES, TILES, LOAD_TILES):
             nc.sync.dma_start(
                 out=h_rows[:, j0 : j0 + LOAD_TILES, :], in_=h_view[:, j0 : j0 + LOAD_TILES, :]
             )
         bias_all = keep.tile([P, BRANCHES, H], BF16)
-        gain_all = keep.tile([P, BRANCHES, H], BF16)
-        shift_all = keep.tile([P, BRANCHES, H], BF16)
-        for vec_tile, vec in ((bias_all, b_liq), (gain_all, g_liq), (shift_all, beta_liq)):
-            nc.scalar.dma_start(
-                out=vec_tile[:].rearrange("p l o -> p (l o)"),
-                in_=vec.rearrange("l o -> (l o)").partition_broadcast(P),
-            )
+        nc.scalar.dma_start(
+            out=bias_all[:].rearrange("p l o -> p (l o)"),
+            in_=b_liq.rearrange("l o -> (l o)").partition_broadcast(P),
+        )
+        vec_rows = keep.tile([P, P], BF16)
+        nc.vector.memset(vec_rows[:], 0.0)
+        nc.scalar.dma_start(
+            out=vec_rows[0:UNITS, :], in_=g_liq.rearrange("l (c p) -> (l c) p", p=P)
+        )
+        nc.scalar.dma_start(
+            out=vec_rows[UNITS : 2 * UNITS, :], in_=beta_liq.rearrange("l (c p) -> (l c) p", p=P)
+        )
 
         ident = keep.tile([P, P], F32)
         make_identity(nc, ident[:])
         eps = keep.tile([P, 1], F32)
         nc.vector.memset(eps[:], LN_EPS)
 
-        shift_sum = keep.tile([P, H], F32)
-        nc.vector.tensor_tensor(
-            out=shift_sum[:], in0=shift_all[:, 0, :], in1=shift_all[:, 1, :], op=ALU.add
-        )
-        nc.vector.tensor_tensor(
-            out=shift_sum[:], in0=shift_sum[:], in1=shift_all[:, 2, :], op=ALU.add
-        )
-
         w_words = w_rows[:].bitcast(F32)
         w_codes = keep.tile([P, BRANCHES, H], U32, align_bytes=64)
         w_scales = keep.tile([P, BRANCHES, H], U8, align_bytes=64)
-        for l in range(BRANCHES):
-            w_grouped = stage.tile([P, H, 4], BF16, align_bytes=64)
+
+        def quantise_weights(l):
+            w_grouped = pairs.tile([P, H, 4], BF16, align_bytes=64)
             w_grouped_words = w_grouped[:].bitcast(F32)
             for half in range(2):
                 w_bank = flip.tile([P, 2, 2 * P], F32, tag="bank")
                 for c in range(2):
                     transpose_words(
-                        nc, w_bank, c * P, w_words[:, l * O_CHUNKS + 2 * half + c, :], ident
+                        nc, w_bank, c * P, w_words[:, l * CHUNKS + 2 * half + c, :], ident
                     )
                 nc.scalar.copy(
                     out=w_grouped_words[:, half * 2 * P : (half + 1) * 2 * P, :],
@@ -104,36 +105,42 @@ def tile_advancedliquidneuralnetwork_pa_t_kernel(
         h_codes = keep.tile([P, TILES * P], U32, align_bytes=64)
         h_scales = keep.tile([P, TILES * P], U8, align_bytes=64)
 
-        def quantise_two_tiles(j0):
+        grouped = {}
+
+        def group_two_tiles(j0):
             h_bank = flip.tile([P, 2, 2 * P], F32, tag="bank")
             for c in range(2):
                 transpose_words(nc, h_bank, c * P, h_words[:, j0 + c, :], ident)
-            h_grouped = stage.tile([P, 2 * P, 4], BF16, align_bytes=64)
+            h_grouped = pairs.tile([P, 2 * P, 4], BF16, align_bytes=64)
             nc.scalar.copy(
                 out=h_grouped[:].bitcast(F32), in_=h_bank[:].rearrange("p u r -> p r u")
             )
+            grouped[j0] = h_grouped
+
+        def quantise_two_tiles(j0):
             nc.vector.quantize_mx(
                 out=h_codes[:, j0 * P : (j0 + 2) * P].bitcast(FP8X4),
                 scales=h_scales[:, j0 * P : (j0 + 2) * P],
-                in_=h_grouped[:].rearrange("p r t -> p (r t)"),
+                in_=grouped[j0][:].rearrange("p r t -> p (r t)"),
             )
 
-        for j in range(TILES):
-            if j % 2 == 0:
-                quantise_two_tiles(j)
-            if j % STORE_TILES == 0:
-                result = work.tile([P, STORE_TILES, H], F32)
+        products = {}
+        resids = {}
+        normed = {}
+        stats = {}
+        summed = {}
+        results = {}
 
-            resid = work.tile([P, BRANCHES, H], F32)
-            nc.vector.tensor_tensor(
+        def multiply(j):
+            resid = pairs.tile([P, BRANCHES, H], F32)
+            nc.gpsimd.tensor_tensor(
                 out=resid[:],
                 in0=h_rows[:, j, :].unsqueeze(1).to_broadcast([P, BRANCHES, H]),
                 in1=bias_all[:],
                 op=ALU.add,
             )
-
-            pre = work.tile([P, BRANCHES, H], F32)
-            row_sum = small.tile([P, BRANCHES], F32)
+            resids[j] = resid
+            products[j] = []
             for l in range(BRANCHES):
                 lin = prod.tile([P, H], F32)
                 nc.tensor.matmul_mx(
@@ -145,27 +152,38 @@ def tile_advancedliquidneuralnetwork_pa_t_kernel(
                     start=True,
                     stop=True,
                 )
+                products[j].append(lin)
+
+        def add_residual(j):
+            if j % QUAD == 0:
+                normed_quad = triples.tile([P, QUAD, BRANCHES, H], F32)
+                normed[j // QUAD] = normed_quad
+            pre = normed[j // QUAD][:, j % QUAD, :, :]
+            row_sum = small.tile([P, BRANCHES], F32)
+            for l in range(BRANCHES):
                 nc.vector.scalar_tensor_tensor(
                     out=pre[:, l, :],
-                    in0=lin[:],
+                    in0=products[j][l][:],
                     scalar=0.0,
-                    in1=resid[:, l, :],
+                    in1=resids[j][:, l, :],
                     op0=ALU.add,
                     op1=ALU.add,
                     accum_out=row_sum[:, l : l + 1],
                 )
-
             neg_mean = small.tile([P, BRANCHES], F32)
             nc.vector.tensor_scalar_mul(out=neg_mean[:], in0=row_sum[:], scalar1=-1.0 / H)
+            stats[j] = {"neg_mean": neg_mean}
 
+        def deviation(j):
+            pre = normed[j // QUAD][:, j % QUAD, :, :]
             sq_sum = small.tile([P, BRANCHES], F32)
             for l in range(BRANCHES):
-                squares = work.tile([P, H], F32)
+                squares = triples.tile([P, H], F32)
                 nc.scalar.activation(
                     out=squares[:],
                     in_=pre[:, l, :],
                     func=ACT.Square,
-                    bias=neg_mean[:, l : l + 1],
+                    bias=stats[j]["neg_mean"][:, l : l + 1],
                     scale=1.0,
                     accum_out=sq_sum[:, l : l + 1],
                 )
@@ -173,30 +191,124 @@ def tile_advancedliquidneuralnetwork_pa_t_kernel(
             nc.scalar.activation(
                 out=std[:], in_=sq_sum[:], func=ACT.Sqrt, bias=eps[:], scale=1.0 / H
             )
-            inv_std = small.tile([P, BRANCHES], F32)
-            nc.vector.reciprocal(out=inv_std[:], in_=std[:])
+            stats[j]["std"] = std
 
-            total = shift_sum[:]
+        def scale_and_offset(j):
+            inv_std = small.tile([P, BRANCHES], F32)
+            nc.vector.reciprocal(out=inv_std[:], in_=stats[j]["std"][:])
+            offset = small.tile([P, BRANCHES], F32)
+            nc.vector.tensor_tensor(
+                out=offset[:], in0=stats[j]["neg_mean"][:], in1=inv_std[:], op=ALU.mult
+            )
+            stats[j]["inv_std"] = inv_std
+            stats[j]["offset"] = offset
+
+        def normalise(j):
+            pre = normed[j // QUAD][:, j % QUAD, :, :]
             for l in range(BRANCHES):
-                gained = work.tile([P, H], F32)
-                nc.vector.scalar_tensor_tensor(
-                    out=gained[:],
-                    in0=pre[:, l, :],
-                    scalar=neg_mean[:, l : l + 1],
-                    in1=gain_all[:, l, :],
-                    op0=ALU.add,
-                    op1=ALU.mult,
+                nc.scalar.activation(
+                    out=pre[:, l, :],
+                    in_=pre[:, l, :],
+                    func=ACT.Identity,
+                    bias=stats[j]["offset"][:, l : l + 1],
+                    scale=stats[j]["inv_std"][:, l : l + 1],
                 )
-                nc.vector.scalar_tensor_tensor(
-                    out=result[:, j % STORE_TILES, :],
-                    in0=gained[:],
-                    scalar=inv_std[:, l : l + 1],
-                    in1=total,
+
+        def gain_and_sum(s, unit):
+            l, c = unit // CHUNKS, unit % CHUNKS
+            if unit == 0:
+                summed_quad = pairs.tile([P, CHUNKS, QUAD * P], F32)
+                summed[s] = summed_quad
+            flipped = cols.tile([P, QUAD * P], F32)
+            for q in range(QUAD):
+                nc.tensor.transpose(
+                    flipped[:, q * P : (q + 1) * P],
+                    normed[s][:, q, l, c * P : (c + 1) * P],
+                    ident[:],
+                )
+            if l == 0:
+                nc.vector.tensor_scalar(
+                    out=summed[s][:, c, :],
+                    in0=flipped[:],
+                    scalar1=vec_cols[:, unit : unit + 1],
+                    scalar2=shift_cols[:, c : c + 1],
                     op0=ALU.mult,
                     op1=ALU.add,
                 )
-                total = result[:, j % STORE_TILES, :]
+            else:
+                nc.vector.scalar_tensor_tensor(
+                    out=summed[s][:, c, :],
+                    in0=flipped[:],
+                    scalar=vec_cols[:, unit : unit + 1],
+                    in1=summed[s][:, c, :],
+                    op0=ALU.mult,
+                    op1=ALU.add,
+                )
 
-            if j % STORE_TILES == STORE_TILES - 1:
-                j0 = j - (STORE_TILES - 1)
-                nc.sync.dma_start(out=out_view[:, j0 : j + 1, :], in_=result[:])
+        def back_to_rows(s, q):
+            if q == 0:
+                result = pairs.tile([P, QUAD, H], F32)
+                results[s] = result
+            back = flip.tile([P, H], F32, tag="bank")
+            for c in range(CHUNKS):
+                nc.tensor.transpose(
+                    back[:, c * P : (c + 1) * P], summed[s][:, c, q * P : (q + 1) * P], ident[:]
+                )
+            if q % 2 == 0:
+                nc.scalar.copy(out=results[s][:, q, :], in_=back[:])
+            else:
+                nc.vector.tensor_copy(out=results[s][:, q, :], in_=back[:])
+            if q == QUAD - 1:
+                nc.sync.dma_start(
+                    out=out_view[:, s * QUAD : (s + 1) * QUAD, :], in_=results[s][:]
+                )
+
+        quantise_weights(0)
+        group_two_tiles(0)
+        quantise_two_tiles(0)
+        quantise_weights(1)
+        quantise_weights(2)
+        multiply(0)
+
+        vec_rows_f32 = keep.tile([P, P], F32)
+        nc.vector.tensor_copy(out=vec_rows_f32[:], in_=vec_rows[:])
+        vec_bank = flip.tile([P, P], F32, tag="bank")
+        nc.tensor.transpose(vec_bank[:], vec_rows_f32[:], ident[:])
+        vec_cols = keep.tile([P, P], F32)
+        nc.vector.tensor_copy(out=vec_cols[:], in_=vec_bank[:])
+        shift_cols = keep.tile([P, CHUNKS], F32)
+        nc.vector.tensor_tensor(
+            out=shift_cols[:],
+            in0=vec_cols[:, UNITS : UNITS + CHUNKS],
+            in1=vec_cols[:, UNITS + CHUNKS : UNITS + 2 * CHUNKS],
+            op=ALU.add,
+        )
+        nc.vector.tensor_tensor(
+            out=shift_cols[:],
+            in0=shift_cols[:],
+            in1=vec_cols[:, UNITS + 2 * CHUNKS : UNITS + 3 * CHUNKS],
+            op=ALU.add,
+        )
+
+        for t in range(STEPS):
+            if 0 <= t - NORM_LAG < TILES:
+                scale_and_offset(t - NORM_LAG)
+            if t % 2 == 1 and t + 1 < TILES:
+                quantise_two_tiles(t + 1)
+            if t < TILES:
+                add_residual(t)
+            if 0 <= t - FLIP_LAG < TILES:
+                for i in range(UNITS_PER_STEP):
+                    gain_and_sum(
+                        (t - FLIP_LAG) // QUAD, ((t - FLIP_LAG) % QUAD) * UNITS_PER_STEP + i
+                    )
+            if t + 1 < TILES:
+                multiply(t + 1)
+            if 0 <= t - 1 < TILES:
+                deviation(t - 1)
+            if 0 <= t - NORM_LAG < TILES:
+                normalise(t - NORM_LAG)
+            if 0 <= t - BACK_LAG < TILES:
+                back_to_rows((t - BACK_LAG) // QUAD, (t - BACK_LAG) % QUAD)
+            if t % 2 == 0 and t + 2 < TILES:
+                group_two_tiles(t + 2)

@@ -133,12 +133,10 @@ def tile_advancedliquidneuralnetwork_pa_t_kernel(
 
         def multiply(j):
             resid = pairs.tile([P, BRANCHES, H], F32)
-            nc.gpsimd.tensor_tensor(
-                out=resid[:],
-                in0=h_rows[:, j, :].unsqueeze(1).to_broadcast([P, BRANCHES, H]),
-                in1=bias_all[:],
-                op=ALU.add,
-            )
+            for l in range(BRANCHES):
+                nc.gpsimd.tensor_tensor(
+                    out=resid[:, l, :], in0=h_rows[:, j, :], in1=bias_all[:, l, :], op=ALU.add
+                )
             resids[j] = resid
             products[j] = []
             for l in range(BRANCHES):

@@ -112,7 +112,7 @@ def tile_advancedliquidneuralnetwork_pa_t_kernel(
             for c in range(2):
                 transpose_words(nc, h_bank, c * P, h_words[:, j0 + c, :], ident)
             h_grouped = pairs.tile([P, 2 * P, 4], BF16, align_bytes=64)
-            nc.scalar.copy(
+            nc.vector.tensor_copy(
                 out=h_grouped[:].bitcast(F32), in_=h_bank[:].rearrange("p u r -> p r u")
             )
             grouped[j0] = h_grouped
@@ -168,12 +168,13 @@ def tile_advancedliquidneuralnetwork_pa_t_kernel(
                     op1=ALU.add,
                     accum_out=row_sum[:, l : l + 1],
                 )
-            neg_mean = small.tile([P, BRANCHES], F32)
-            nc.vector.tensor_scalar_mul(out=neg_mean[:], in0=row_sum[:], scalar1=-1.0 / H)
-            stats[j] = {"neg_mean": neg_mean}
+            stats[j] = {"row_sum": row_sum}
 
         def deviation(j):
             pre = normed[j // QUAD][:, j % QUAD, :, :]
+            neg_mean = small.tile([P, BRANCHES], F32)
+            nc.scalar.mul(out=neg_mean[:], in_=stats[j]["row_sum"][:], mul=-1.0 / H)
+            stats[j]["neg_mean"] = neg_mean
             sq_sum = small.tile([P, BRANCHES], F32)
             for l in range(BRANCHES):
                 squares = triples.tile([P, H], F32)
@@ -185,21 +186,34 @@ def tile_advancedliquidneuralnetwork_pa_t_kernel(
                     scale=1.0,
                     accum_out=sq_sum[:, l : l + 1],
                 )
-            std = small.tile([P, BRANCHES], F32)
-            nc.scalar.activation(
-                out=std[:], in_=sq_sum[:], func=ACT.Sqrt, bias=eps[:], scale=1.0 / H
-            )
-            stats[j]["std"] = std
-
-        def scale_and_offset(j):
             inv_std = small.tile([P, BRANCHES], F32)
-            nc.vector.reciprocal(out=inv_std[:], in_=stats[j]["std"][:])
-            offset = small.tile([P, BRANCHES], F32)
-            nc.vector.tensor_tensor(
-                out=offset[:], in0=stats[j]["neg_mean"][:], in1=inv_std[:], op=ALU.mult
+            nc.scalar.activation(
+                out=inv_std[:],
+                in_=sq_sum[:],
+                func=ACT.Abs_reciprocal_sqrt,
+                bias=eps[:],
+                scale=1.0 / H,
             )
             stats[j]["inv_std"] = inv_std
+
+        def offsets(j):
+            offset = small.tile([P, BRANCHES], F32)
+            nc.gpsimd.tensor_tensor(
+                out=offset[:], in0=stats[j]["neg_mean"][:], in1=stats[j]["inv_std"][:], op=ALU.mult
+            )
             stats[j]["offset"] = offset
+
+        def normalise_on_vector(j):
+            pre = normed[j // QUAD][:, j % QUAD, :, :]
+            for l in range(BRANCHES):
+                nc.vector.tensor_scalar(
+                    out=pre[:, l, :],
+                    in0=pre[:, l, :],
+                    scalar1=stats[j]["neg_mean"][:, l : l + 1],
+                    scalar2=stats[j]["inv_std"][:, l : l + 1],
+                    op0=ALU.add,
+                    op1=ALU.mult,
+                )
 
         def normalise(j):
             pre = normed[j // QUAD][:, j % QUAD, :, :]
@@ -243,7 +257,7 @@ def tile_advancedliquidneuralnetwork_pa_t_kernel(
                     op1=ALU.add,
                 )
 
-        def back_to_rows(s, q):
+        def back_to_rows(s, q, scalar_is_idle):
             if q == 0:
                 result = pairs.tile([P, QUAD, H], F32)
                 results[s] = result
@@ -252,14 +266,11 @@ def tile_advancedliquidneuralnetwork_pa_t_kernel(
                 nc.tensor.transpose(
                     back[:, c * P : (c + 1) * P], summed[s][:, c, q * P : (q + 1) * P], ident[:]
                 )
-            if q % 2 == 0:
+            if q % 2 == 0 or scalar_is_idle:
                 nc.scalar.copy(out=results[s][:, q, :], in_=back[:])
             else:
                 nc.vector.tensor_copy(out=results[s][:, q, :], in_=back[:])
-            if q == QUAD - 1:
-                nc.sync.dma_start(
-                    out=out_view[:, s * QUAD : (s + 1) * QUAD, :], in_=results[s][:]
-                )
+            nc.sync.dma_start(out=out_view[:, s * QUAD + q, :], in_=results[s][:, q, :])
 
         quantise_weights(0)
         group_two_tiles(0)
@@ -289,8 +300,8 @@ def tile_advancedliquidneuralnetwork_pa_t_kernel(
         )
 
         for t in range(STEPS):
-            if 0 <= t - NORM_LAG < TILES:
-                scale_and_offset(t - NORM_LAG)
+            if QUAD <= t - NORM_LAG < TILES:
+                offsets(t - NORM_LAG)
             if t % 2 == 1 and t + 1 < TILES:
                 quantise_two_tiles(t + 1)
             if t < TILES:
@@ -304,9 +315,13 @@ def tile_advancedliquidneuralnetwork_pa_t_kernel(
                 multiply(t + 1)
             if 0 <= t - 1 < TILES:
                 deviation(t - 1)
-            if 0 <= t - NORM_LAG < TILES:
+            if 0 <= t - NORM_LAG < QUAD:
+                normalise_on_vector(t - NORM_LAG)
+            if QUAD <= t - NORM_LAG < TILES:
                 normalise(t - NORM_LAG)
             if 0 <= t - BACK_LAG < TILES:
-                back_to_rows((t - BACK_LAG) // QUAD, (t - BACK_LAG) % QUAD)
+                back_to_rows(
+                    (t - BACK_LAG) // QUAD, (t - BACK_LAG) % QUAD, t - NORM_LAG >= TILES
+                )
             if t % 2 == 0 and t + 2 < TILES:
                 group_two_tiles(t + 2)

@@ -20,6 +20,7 @@ LOAD_TILES = 8
 UNITS = BRANCHES * CHUNKS
 UNITS_PER_STEP = UNITS // QUAD
 NORM_LAG = 2
+RESID_AHEAD = 3
 FLIP_LAG = QUAD - 1 + NORM_LAG + 1
 BACK_LAG = FLIP_LAG + QUAD
 STEPS = TILES + BACK_LAG
@@ -45,8 +46,8 @@ def tile_advancedliquidneuralnetwork_pa_t_kernel(
     with tc.tile_pool(name="keep", bufs=1) as keep, tc.tile_pool(
         name="pairs", bufs=2
     ) as pairs, tc.tile_pool(name="triples", bufs=3) as triples, tc.tile_pool(
-        name="small", bufs=6
-    ) as small, tc.psum_pool(name="flip", bufs=2) as flip, tc.psum_pool(
+        name="ahead", bufs=RESID_AHEAD + 1
+    ) as ahead, tc.tile_pool(name="small", bufs=6) as small, tc.psum_pool(name="flip", bufs=2) as flip, tc.psum_pool(
         name="prod", bufs=BRANCHES
     ) as prod, tc.psum_pool(name="cols", bufs=UNITS_PER_STEP) as cols, tc.manual_schedule():
         w_rows = keep.tile([P, UNITS, H], BF16)
@@ -131,13 +132,15 @@ def tile_advancedliquidneuralnetwork_pa_t_kernel(
         summed = {}
         results = {}
 
-        def multiply(j):
-            resid = pairs.tile([P, BRANCHES, H], F32)
+        def residual_input(j):
+            resid = ahead.tile([P, BRANCHES, H], F32)
             for l in range(BRANCHES):
                 nc.gpsimd.tensor_tensor(
                     out=resid[:, l, :], in0=h_rows[:, j, :], in1=bias_all[:, l, :], op=ALU.add
                 )
             resids[j] = resid
+
+        def multiply(j):
             products[j] = []
             for l in range(BRANCHES):
                 lin = prod.tile([P, H], F32)
@@ -198,9 +201,12 @@ def tile_advancedliquidneuralnetwork_pa_t_kernel(
 
         def offsets(j):
             offset = small.tile([P, BRANCHES], F32)
-            nc.gpsimd.tensor_tensor(
-                out=offset[:], in0=stats[j]["neg_mean"][:], in1=stats[j]["inv_std"][:], op=ALU.mult
-            )
+            for l in range(BRANCHES):
+                nc.scalar.mul(
+                    out=offset[:, l : l + 1],
+                    in_=stats[j]["neg_mean"][:, l : l + 1],
+                    mul=stats[j]["inv_std"][:, l : l + 1],
+                )
             stats[j]["offset"] = offset
 
         def normalise_on_vector(j):
@@ -272,6 +278,8 @@ def tile_advancedliquidneuralnetwork_pa_t_kernel(
                 nc.vector.tensor_copy(out=results[s][:, q, :], in_=back[:])
             nc.sync.dma_start(out=out_view[:, s * QUAD + q, :], in_=results[s][:, q, :])
 
+        for j in range(RESID_AHEAD):
+            residual_input(j)
         quantise_weights(0)
         group_two_tiles(0)
         quantise_two_tiles(0)
@@ -300,8 +308,6 @@ def tile_advancedliquidneuralnetwork_pa_t_kernel(
         )
 
         for t in range(STEPS):
-            if QUAD <= t - NORM_LAG < TILES:
-                offsets(t - NORM_LAG)
             if t % 2 == 1 and t + 1 < TILES:
                 quantise_two_tiles(t + 1)
             if t < TILES:
@@ -311,6 +317,8 @@ def tile_advancedliquidneuralnetwork_pa_t_kernel(
                     gain_and_sum(
                         (t - FLIP_LAG) // QUAD, ((t - FLIP_LAG) % QUAD) * UNITS_PER_STEP + i
                     )
+            if t + RESID_AHEAD < TILES:
+                residual_input(t + RESID_AHEAD)
             if t + 1 < TILES:
                 multiply(t + 1)
             if 0 <= t - 1 < TILES:
@@ -318,6 +326,7 @@ def tile_advancedliquidneuralnetwork_pa_t_kernel(
             if 0 <= t - NORM_LAG < QUAD:
                 normalise_on_vector(t - NORM_LAG)
             if QUAD <= t - NORM_LAG < TILES:
+                offsets(t - NORM_LAG)
                 normalise(t - NORM_LAG)
             if 0 <= t - BACK_LAG < TILES:
                 back_to_rows(

@@ -20,7 +20,6 @@ LOAD_TILES = 8
 UNITS = BRANCHES * CHUNKS
 UNITS_PER_STEP = UNITS // QUAD
 NORM_LAG = 2
-RESID_AHEAD = 3
 FLIP_LAG = QUAD - 1 + NORM_LAG + 1
 BACK_LAG = FLIP_LAG + QUAD
 STEPS = TILES + BACK_LAG
@@ -46,8 +45,8 @@ def tile_advancedliquidneuralnetwork_pa_t_kernel(
     with tc.tile_pool(name="keep", bufs=1) as keep, tc.tile_pool(
         name="pairs", bufs=2
     ) as pairs, tc.tile_pool(name="triples", bufs=3) as triples, tc.tile_pool(
-        name="ahead", bufs=RESID_AHEAD + 1
-    ) as ahead, tc.tile_pool(name="small", bufs=6) as small, tc.psum_pool(name="flip", bufs=2) as flip, tc.psum_pool(
+        name="small", bufs=6
+    ) as small, tc.psum_pool(name="flip", bufs=2) as flip, tc.psum_pool(
         name="prod", bufs=BRANCHES
     ) as prod, tc.psum_pool(name="cols", bufs=UNITS_PER_STEP) as cols, tc.manual_schedule():
         w_rows = keep.tile([P, UNITS, H], BF16)
@@ -132,15 +131,13 @@ def tile_advancedliquidneuralnetwork_pa_t_kernel(
         summed = {}
         results = {}
 
-        def residual_input(j):
-            resid = ahead.tile([P, BRANCHES, H], F32)
+        def multiply(j):
+            resid = pairs.tile([P, BRANCHES, H], F32)
             for l in range(BRANCHES):
                 nc.gpsimd.tensor_tensor(
                     out=resid[:, l, :], in0=h_rows[:, j, :], in1=bias_all[:, l, :], op=ALU.add
                 )
             resids[j] = resid
-
-        def multiply(j):
             products[j] = []
             for l in range(BRANCHES):
                 lin = prod.tile([P, H], F32)
@@ -201,12 +198,9 @@ def tile_advancedliquidneuralnetwork_pa_t_kernel(
 
         def offsets(j):
             offset = small.tile([P, BRANCHES], F32)
-            for l in range(BRANCHES):
-                nc.scalar.mul(
-                    out=offset[:, l : l + 1],
-                    in_=stats[j]["neg_mean"][:, l : l + 1],
-                    mul=stats[j]["inv_std"][:, l : l + 1],
-                )
+            nc.gpsimd.tensor_tensor(
+                out=offset[:], in0=stats[j]["neg_mean"][:], in1=stats[j]["inv_std"][:], op=ALU.mult
+            )
             stats[j]["offset"] = offset
 
         def normalise_on_vector(j):
@@ -272,14 +266,12 @@ def tile_advancedliquidneuralnetwork_pa_t_kernel(
                 nc.tensor.transpose(
                     back[:, c * P : (c + 1) * P], summed[s][:, c, q * P : (q + 1) * P], ident[:]
                 )
-            if q % 2 == 0 or scalar_is_idle:
+            if scalar_is_idle:
                 nc.scalar.copy(out=results[s][:, q, :], in_=back[:])
             else:
                 nc.vector.tensor_copy(out=results[s][:, q, :], in_=back[:])
             nc.sync.dma_start(out=out_view[:, s * QUAD + q, :], in_=results[s][:, q, :])
 
-        for j in range(RESID_AHEAD):
-            residual_input(j)
         quantise_weights(0)
         group_two_tiles(0)
         quantise_two_tiles(0)
@@ -308,6 +300,8 @@ def tile_advancedliquidneuralnetwork_pa_t_kernel(
         )
 
         for t in range(STEPS):
+            if QUAD <= t - NORM_LAG < TILES:
+                offsets(t - NORM_LAG)
             if t % 2 == 1 and t + 1 < TILES:
                 quantise_two_tiles(t + 1)
             if t < TILES:
@@ -317,8 +311,6 @@ def tile_advancedliquidneuralnetwork_pa_t_kernel(
                     gain_and_sum(
                         (t - FLIP_LAG) // QUAD, ((t - FLIP_LAG) % QUAD) * UNITS_PER_STEP + i
                     )
-            if t + RESID_AHEAD < TILES:
-                residual_input(t + RESID_AHEAD)
             if t + 1 < TILES:
                 multiply(t + 1)
             if 0 <= t - 1 < TILES:
@@ -326,7 +318,6 @@ def tile_advancedliquidneuralnetwork_pa_t_kernel(
             if 0 <= t - NORM_LAG < QUAD:
                 normalise_on_vector(t - NORM_LAG)
             if QUAD <= t - NORM_LAG < TILES:
-                offsets(t - NORM_LAG)
                 normalise(t - NORM_LAG)
             if 0 <= t - BACK_LAG < TILES:
                 back_to_rows(

import concourse.mybir as mybir
from concourse.masks import make_identity

F32 = mybir.dt.float32
BF16 = mybir.dt.bfloat16
U32 = mybir.dt.uint32
U8 = mybir.dt.uint8
FP8X4 = mybir.dt.float8_e4m3fn_x4
ALU = mybir.AluOpType
ACT = mybir.ActivationFunctionType

P = 128
ROWS = 4096
H = 512
BRANCHES = 3
TILES = ROWS // P
CHUNKS = H // P
QUAD = 4
LOAD_TILES = 8
UNITS = BRANCHES * CHUNKS
UNITS_PER_STEP = UNITS // QUAD
NORM_LAG = 2
FLIP_LAG = QUAD - 1 + NORM_LAG + 1
BACK_LAG = FLIP_LAG + QUAD
STEPS = TILES + BACK_LAG
LN_EPS = 1e-5

FLOPS = 2 * ROWS * H * H * BRANCHES


def transpose_words(nc, bank, column, words, ident):
    for u in range(2):
        nc.tensor.transpose(
            bank[:, u, column : column + P], words[:, u * P : (u + 1) * P], ident[:]
        )


def tile_advancedliquidneuralnetwork_pa_t_kernel(
    tc, h, W_liq, b_liq, g_liq, beta_liq, out
):
    nc = tc.nc
    h_view = h.rearrange("(p j) k -> p j k", j=TILES)
    out_view = out.rearrange("(p j) o -> p j o", j=TILES)

    with tc.tile_pool(name="keep", bufs=1) as keep, tc.tile_pool(
        name="pairs", bufs=2
    ) as pairs, tc.tile_pool(name="triples", bufs=3) as triples, tc.tile_pool(
        name="small", bufs=6
    ) as small, tc.psum_pool(name="flip", bufs=2) as flip, tc.psum_pool(
        name="prod", bufs=BRANCHES
    ) as prod, tc.psum_pool(name="cols", bufs=UNITS_PER_STEP) as cols, tc.manual_schedule():
        w_rows = keep.tile([P, UNITS, H], BF16)
        h_rows = keep.tile([P, TILES, H], BF16)
        w_view = W_liq.rearrange("l (c p) k -> p (l c) k", p=P)
        nc.sync.dma_start(out=w_rows[:, 0:CHUNKS, :], in_=w_view[:, 0:CHUNKS, :])
        nc.sync.dma_start(out=h_rows[:, 0:LOAD_TILES, :], in_=h_view[:, 0:LOAD_TILES, :])
        nc.sync.dma_start(out=w_rows[:, CHUNKS:, :], in_=w_view[:, CHUNKS:, :])
        for j0 in range(LOAD_TILES, TILES, LOAD_TILES):
            nc.sync.dma_start(
                out=h_rows[:, j0 : j0 + LOAD_TILES, :], in_=h_view[:, j0 : j0 + LOAD_TILES, :]
            )
        bias_all = keep.tile([P, BRANCHES, H], BF16)
        nc.scalar.dma_start(
            out=bias_all[:].rearrange("p l o -> p (l o)"),
            in_=b_liq.rearrange("l o -> (l o)").partition_broadcast(P),
        )
        vec_rows = keep.tile([P, P], BF16)
        nc.vector.memset(vec_rows[:], 0.0)
        nc.scalar.dma_start(
            out=vec_rows[0:UNITS, :], in_=g_liq.rearrange("l (c p) -> (l c) p", p=P)
        )
        nc.scalar.dma_start(
            out=vec_rows[UNITS : 2 * UNITS, :], in_=beta_liq.rearrange("l (c p) -> (l c) p", p=P)
        )

        ident = keep.tile([P, P], F32)
        make_identity(nc, ident[:])
        eps = keep.tile([P, 1], F32)
        nc.vector.memset(eps[:], LN_EPS)

        w_words = w_rows[:].bitcast(F32)
        w_codes = keep.tile([P, BRANCHES, H], U32, align_bytes=64)
        w_scales = keep.tile([P, BRANCHES, H], U8, align_bytes=64)

        def quantise_weights(l):
            w_grouped = pairs.tile([P, H, 4], BF16, align_bytes=64)
            w_grouped_words = w_grouped[:].bitcast(F32)
            for half in range(2):
                w_bank = flip.tile([P, 2, 2 * P], F32, tag="bank")
                for c in range(2):
                    transpose_words(
                        nc, w_bank, c * P, w_words[:, l * CHUNKS + 2 * half + c, :], ident
                    )
                nc.scalar.copy(
                    out=w_grouped_words[:, half * 2 * P : (half + 1) * 2 * P, :],
                    in_=w_bank[:].rearrange("p u o -> p o u"),
                )
            nc.vector.quantize_mx(
                out=w_codes[:, l, :].bitcast(FP8X4),
                scales=w_scales[:, l, :],
                in_=w_grouped[:].rearrange("p o t -> p (o t)"),
            )

        h_words = h_rows[:].bitcast(F32)
        h_codes = keep.tile([P, TILES * P], U32, align_bytes=64)
        h_scales = keep.tile([P, TILES * P], U8, align_bytes=64)

        grouped = {}

        def group_two_tiles(j0):
            h_bank = flip.tile([P, 2, 2 * P], F32, tag="bank")
            for c in range(2):
                transpose_words(nc, h_bank, c * P, h_words[:, j0 + c, :], ident)
            h_grouped = pairs.tile([P, 2 * P, 4], BF16, align_bytes=64)
            nc.vector.tensor_copy(
                out=h_grouped[:].bitcast(F32), in_=h_bank[:].rearrange("p u r -> p r u")
            )
            grouped[j0] = h_grouped

        def quantise_two_tiles(j0):
            nc.vector.quantize_mx(
                out=h_codes[:, j0 * P : (j0 + 2) * P].bitcast(FP8X4),
                scales=h_scales[:, j0 * P : (j0 + 2) * P],
                in_=grouped[j0][:].rearrange("p r t -> p (r t)"),
            )

        products = {}
        resids = {}
        normed = {}
        stats = {}
        summed = {}
        results = {}

        def multiply(j):
            resid = pairs.tile([P, BRANCHES, H], F32)
            for l in range(BRANCHES):
                nc.gpsimd.tensor_tensor(
                    out=resid[:, l, :], in0=h_rows[:, j, :], in1=bias_all[:, l, :], op=ALU.add
                )
            resids[j] = resid
            products[j] = []
            for l in range(BRANCHES):
                lin = prod.tile([P, H], F32)
                nc.tensor.matmul_mx(
                    out=lin[:],
                    lhsT=h_codes[:, j * P : (j + 1) * P].bitcast(FP8X4),
                    lhsT_scale=h_scales[:, j * P : (j + 1) * P],
                    rhs=w_codes[:, l, :].bitcast(FP8X4),
                    rhs_scale=w_scales[:, l, :],
                    start=True,
                    stop=True,
                )
                products[j].append(lin)

        def add_residual(j):
            if j % QUAD == 0:
                normed_quad = triples.tile([P, QUAD, BRANCHES, H], F32)
                normed[j // QUAD] = normed_quad
            pre = normed[j // QUAD][:, j % QUAD, :, :]
            row_sum = small.tile([P, BRANCHES], F32)
            for l in range(BRANCHES):
                nc.vector.scalar_tensor_tensor(
                    out=pre[:, l, :],
                    in0=products[j][l][:],
                    scalar=0.0,
                    in1=resids[j][:, l, :],
                    op0=ALU.add,
                    op1=ALU.add,
                    accum_out=row_sum[:, l : l + 1],
                )
            stats[j] = {"row_sum": row_sum}

        def deviation(j):
            pre = normed[j // QUAD][:, j % QUAD, :, :]
            neg_mean = small.tile([P, BRANCHES], F32)
            nc.scalar.mul(out=neg_mean[:], in_=stats[j]["row_sum"][:], mul=-1.0 / H)
            stats[j]["neg_mean"] = neg_mean
            sq_sum = small.tile([P, BRANCHES], F32)
            for l in range(BRANCHES):
                squares = triples.tile([P, H], F32)
                nc.scalar.activation(
                    out=squares[:],
                    in_=pre[:, l, :],
                    func=ACT.Square,
                    bias=stats[j]["neg_mean"][:, l : l + 1],
                    scale=1.0,
                    accum_out=sq_sum[:, l : l + 1],
                )
            inv_std = small.tile([P, BRANCHES], F32)
            nc.scalar.activation(
                out=inv_std[:],
                in_=sq_sum[:],
                func=ACT.Abs_reciprocal_sqrt,
                bias=eps[:],
                scale=1.0 / H,
            )
            stats[j]["inv_std"] = inv_std

        def offsets(j):
            offset = small.tile([P, BRANCHES], F32)
            nc.gpsimd.tensor_tensor(
                out=offset[:], in0=stats[j]["neg_mean"][:], in1=stats[j]["inv_std"][:], op=ALU.mult
            )
            stats[j]["offset"] = offset

        def normalise_on_vector(j):
            pre = normed[j // QUAD][:, j % QUAD, :, :]
            for l in range(BRANCHES):
                nc.vector.tensor_scalar(
                    out=pre[:, l, :],
                    in0=pre[:, l, :],
                    scalar1=stats[j]["neg_mean"][:, l : l + 1],
                    scalar2=stats[j]["inv_std"][:, l : l + 1],
                    op0=ALU.add,
                    op1=ALU.mult,
                )

        def normalise(j):
            pre = normed[j // QUAD][:, j % QUAD, :, :]
            for l in range(BRANCHES):
                nc.scalar.activation(
                    out=pre[:, l, :],
                    in_=pre[:, l, :],
                    func=ACT.Identity,
                    bias=stats[j]["offset"][:, l : l + 1],
                    scale=stats[j]["inv_std"][:, l : l + 1],
                )

        def gain_and_sum(s, unit):
            l, c = unit // CHUNKS, unit % CHUNKS
            if unit == 0:
                summed_quad = pairs.tile([P, CHUNKS, QUAD * P], F32)
                summed[s] = summed_quad
            flipped = cols.tile([P, QUAD * P], F32)
            for q in range(QUAD):
                nc.tensor.transpose(
                    flipped[:, q * P : (q + 1) * P],
                    normed[s][:, q, l, c * P : (c + 1) * P],
                    ident[:],
                )
            if l == 0:
                nc.vector.tensor_scalar(
                    out=summed[s][:, c, :],
                    in0=flipped[:],
                    scalar1=vec_cols[:, unit : unit + 1],
                    scalar2=shift_cols[:, c : c + 1],
                    op0=ALU.mult,
                    op1=ALU.add,
                )
            else:
                nc.vector.scalar_tensor_tensor(
                    out=summed[s][:, c, :],
                    in0=flipped[:],
                    scalar=vec_cols[:, unit : unit + 1],
                    in1=summed[s][:, c, :],
                    op0=ALU.mult,
                    op1=ALU.add,
                )

        def back_to_rows(s, q, scalar_is_idle):
            if q == 0:
                result = pairs.tile([P, QUAD, H], F32)
                results[s] = result
            back = flip.tile([P, H], F32, tag="bank")
            for c in range(CHUNKS):
                nc.tensor.transpose(
                    back[:, c * P : (c + 1) * P], summed[s][:, c, q * P : (q + 1) * P], ident[:]
                )
            if scalar_is_idle:
                nc.scalar.copy(out=results[s][:, q, :], in_=back[:])
            else:
                nc.vector.tensor_copy(out=results[s][:, q, :], in_=back[:])
            nc.sync.dma_start(out=out_view[:, s * QUAD + q, :], in_=results[s][:, q, :])

        quantise_weights(0)
        group_two_tiles(0)
        quantise_two_tiles(0)
        quantise_weights(1)
        quantise_weights(2)
        multiply(0)

        vec_rows_f32 = keep.tile([P, P], F32)
        nc.vector.tensor_copy(out=vec_rows_f32[:], in_=vec_rows[:])
        vec_bank = flip.tile([P, P], F32, tag="bank")
        nc.tensor.transpose(vec_bank[:], vec_rows_f32[:], ident[:])
        vec_cols = keep.tile([P, P], F32)
        nc.vector.tensor_copy(out=vec_cols[:], in_=vec_bank[:])
        shift_cols = keep.tile([P, CHUNKS], F32)
        nc.vector.tensor_tensor(
            out=shift_cols[:],
            in0=vec_cols[:, UNITS : UNITS + CHUNKS],
            in1=vec_cols[:, UNITS + CHUNKS : UNITS + 2 * CHUNKS],
            op=ALU.add,
        )
        nc.vector.tensor_tensor(
            out=shift_cols[:],
            in0=shift_cols[:],
            in1=vec_cols[:, UNITS + 2 * CHUNKS : UNITS + 3 * CHUNKS],
            op=ALU.add,
        )

        for t in range(STEPS):
            if QUAD <= t - NORM_LAG < TILES:
                offsets(t - NORM_LAG)
            if t % 2 == 1 and t + 1 < TILES:
                quantise_two_tiles(t + 1)
            if t < TILES:
                add_residual(t)
            if 0 <= t - FLIP_LAG < TILES:
                for i in range(UNITS_PER_STEP):
                    gain_and_sum(
                        (t - FLIP_LAG) // QUAD, ((t - FLIP_LAG) % QUAD) * UNITS_PER_STEP + i
                    )
            if t + 1 < TILES:
                multiply(t + 1)
            if 0 <= t - 1 < TILES:
                deviation(t - 1)
            if 0 <= t - NORM_LAG < QUAD:
                normalise_on_vector(t - NORM_LAG)
            if QUAD <= t - NORM_LAG < TILES:
                normalise(t - NORM_LAG)
            if 0 <= t - BACK_LAG < TILES:
                back_to_rows(
                    (t - BACK_LAG) // QUAD, (t - BACK_LAG) % QUAD, t - NORM_LAG >= TILES
                )
            if t % 2 == 0 and t + 2 < TILES:
                group_two_tiles(t + 2)
